import numpy as np
import ml_dtypes


def mxq(x, axis, fmt="e4m3"):
    dtype, down = {"e4m3": (ml_dtypes.float8_e4m3fn, 7), "e5m2": (ml_dtypes.float8_e5m2, 14)}[fmt]
    v = np.moveaxis(np.asarray(x, np.float32).astype(ml_dtypes.bfloat16).astype(np.float64), axis, -1)
    blocks = v.reshape(v.shape[:-1] + (-1, 32))
    amax = np.abs(blocks).max(-1, keepdims=True)
    byte = np.maximum(np.where(amax > 0, np.frexp(amax)[1] - 1 + 127, 0) - down, 1)
    scale = np.exp2(byte - 127.0)
    codes = (blocks / scale).astype(np.float32).astype(dtype).astype(np.float64)
    return np.moveaxis((codes * scale).reshape(v.shape), -1, axis)


WIDE = False


def mx_kscale(k):
    if not WIDE:
        return np.ones(k)
    levels = np.array([10, -10, 5, -5, 0])
    if k % 512:
        return np.exp2(np.random.permutation(np.resize(levels, k // 32))).repeat(32)
    a = np.empty((k // 512, 16))
    for p in range(k // 512):
        a[p, :8] = np.random.permutation(np.resize(levels, 8))
        for g in range(8):
            far = levels[np.abs(levels - a[p, g]) >= 10]
            a[p, g + 8] = far[np.random.randint(len(far))]
    return np.exp2(a.ravel()).repeat(32)


BF16 = ml_dtypes.bfloat16


def bf(x):
    return np.asarray(x, np.float32).astype(BF16)


def f64(x):
    return np.asarray(x).astype(np.float64)


E2M1 = np.array([0.0, 0.5, 1.0, 1.5, 2.0, 3.0, 4.0, 6.0, -0.0, -0.5, -1.0, -1.5, -2.0, -3.0, -4.0, -6.0])


def pack_weight(w, fmt):
    k, n = w.shape
    w = f64(bf(w)).reshape(k // 32, 32, n)
    amax = np.abs(w).max(1)
    if fmt == "e4m3":
        byte = np.frexp(amax)[1] - 1 + 127 - 7
    else:
        mant, ex = np.frexp(amax / 6.0)
        byte = np.where(mant > 0.5, ex, ex - 1) + 127
    byte = np.clip(np.where(amax > 0, byte, 1), 1, 254)
    scaled = (w * np.exp2(127.0 - byte)[:, None, :]).reshape(k, n).astype(np.float32)
    by_word = np.ascontiguousarray(scaled.reshape(k // 512, 128, 4, n).transpose(0, 1, 3, 2))
    if fmt == "e4m3":
        words = by_word.astype(ml_dtypes.float8_e4m3fn).view(np.uint8)
    else:
        c = by_word.astype(ml_dtypes.float4_e2m1fn).view(np.uint8) & 0xF
        words = c[..., 0::2] | (c[..., 1::2] << 4)
    return np.ascontiguousarray(words), np.ascontiguousarray(byte.astype(np.uint8).reshape(k // 512, 16, n))


def unpack_weight(words, scales, fmt):
    g, p, n, _ = words.shape
    if fmt == "e4m3":
        vals = np.ascontiguousarray(words).view(ml_dtypes.float8_e4m3fn).astype(np.float64)
    else:
        nib = np.empty((g, p, n, 4), np.uint8)
        nib[..., 0::2] = words & 0xF
        nib[..., 1::2] = words >> 4
        vals = E2M1[nib]
    vals = vals * np.repeat(np.exp2(scales.astype(np.float64) - 127.0), 8, axis=1)[..., None]
    return vals.transpose(0, 1, 3, 2).reshape(g * 512, n)


B, S, D, H, DH, L, R = 1, 512, 2048, 16, 128, 1024, 64
DQK = L // 2
C = DH - R
HALF = R // 2


def rope(t):
    inv_freq = 1.0 / (10000.0 ** (np.arange(0, R, 2) / R))
    ang = np.arange(S)[:, None] * inv_freq[None, :]
    cos = np.cos(ang)[None, :, None, :]
    sin = np.sin(ang)[None, :, None, :]
    t1, t2 = t[..., :HALF], t[..., HALF:]
    return np.concatenate([t1 * cos - t2 * sin, t1 * sin + t2 * cos], axis=-1)


def draw0():
    s, t = mx_kscale(D), mx_kscale(DQK)
    x = bf(np.random.standard_normal((B, S, D)) * s)
    W_comp_qk_words, W_comp_qk_scales = pack_weight(np.random.standard_normal((D, DQK)) / np.sqrt(D) / s[:, None] * t, "e4m3")
    W_q_dec_words, W_q_dec_scales = pack_weight(np.random.standard_normal((DQK, H * C)) / np.sqrt(DQK) / t[:, None], "e4m3")
    W_k_dec_words, W_k_dec_scales = pack_weight(np.random.standard_normal((DQK, H * C)) / np.sqrt(DQK) / t[:, None], "e4m3")
    W_rope_q_words, W_rope_q_scales = pack_weight(np.random.standard_normal((D, H * R)) / np.sqrt(D) / s[:, None], "e4m3")
    W_rope_k_words, W_rope_k_scales = pack_weight(np.random.standard_normal((D, H * R)) / np.sqrt(D) / s[:, None], "e4m3")
    return {"x": x,
            "W_comp_qk_words": W_comp_qk_words, "W_comp_qk_scales": W_comp_qk_scales,
            "W_q_dec_words": W_q_dec_words, "W_q_dec_scales": W_q_dec_scales,
            "W_k_dec_words": W_k_dec_words, "W_k_dec_scales": W_k_dec_scales,
            "W_rope_q_words": W_rope_q_words, "W_rope_q_scales": W_rope_q_scales,
            "W_rope_k_words": W_rope_k_words, "W_rope_k_scales": W_rope_k_scales}


def core(x, W_comp_qk_words, W_comp_qk_scales, W_q_dec_words, W_q_dec_scales, W_k_dec_words, W_k_dec_scales,
              W_rope_q_words, W_rope_q_scales, W_rope_k_words, W_rope_k_scales):
    xq = mxq(f64(x), 2, "e4m3")
    c_qk = xq @ unpack_weight(W_comp_qk_words, W_comp_qk_scales, "e4m3")
    cq = mxq(c_qk, 2, "e4m3")
    q_no_rope = cq @ unpack_weight(W_q_dec_words, W_q_dec_scales, "e4m3")
    k_no_rope = cq @ unpack_weight(W_k_dec_words, W_k_dec_scales, "e4m3")
    q_rope = xq @ unpack_weight(W_rope_q_words, W_rope_q_scales, "e4m3")
    k_rope = xq @ unpack_weight(W_rope_k_words, W_rope_k_scales, "e4m3")
    q = np.concatenate([q_no_rope, q_rope], axis=-1).reshape(B, S, H, DH)
    k = np.concatenate([k_no_rope, k_rope], axis=-1).reshape(B, S, H, DH)
    q = np.concatenate([q[..., :C], rope(q[..., C:])], axis=-1)
    k = np.concatenate([k[..., :C], rope(k[..., C:])], axis=-1)
    return q, k


def e4m3fn_bytes(y):
    return np.clip(np.asarray(y, np.float64), -448.0, 448.0).astype(np.float32).astype(ml_dtypes.float8_e4m3fn).view(np.uint8)


def e4m3fn_values(b):
    return np.asarray(b, np.uint8).view(ml_dtypes.float8_e4m3fn).astype(np.float64)


def setup_inputs():
    d = draw0()
    x0 = np.asarray(d['x']).astype(np.float64)
    s = (np.max(np.abs(x0), axis=(0, 1), keepdims=True) / 448.0).astype(np.float32)
    out = {}
    for k, v in d.items():
        if k == 'x':
            out['x_bytes'] = e4m3fn_bytes(x0 / s.astype(np.float64))
            out['x_scale'] = s
        else:
            out[k] = v
    return out


def reference(x_bytes, x_scale, W_comp_qk_words, W_comp_qk_scales, W_q_dec_words, W_q_dec_scales, W_k_dec_words, W_k_dec_scales, W_rope_q_words, W_rope_q_scales, W_rope_k_words, W_rope_k_scales):
    return core(e4m3fn_values(x_bytes) * x_scale.astype(np.float64), W_comp_qk_words, W_comp_qk_scales, W_q_dec_words, W_q_dec_scales, W_k_dec_words, W_k_dec_scales, W_rope_q_words, W_rope_q_scales, W_rope_k_words, W_rope_k_scales)

@@ -1,0 +1,375 @@
+import math
+from contextlib import ExitStack
+
+import concourse.mybir as mybir
+from concourse.masks import make_identity
+
+F32 = mybir.dt.float32
+BF16 = mybir.dt.bfloat16
+I32 = mybir.dt.int32
+U32 = mybir.dt.uint32
+U8 = mybir.dt.uint8
+FP8 = mybir.dt.float8_e4m3fn
+FP8X4 = mybir.dt.float8_e4m3fn_x4
+ALU = mybir.AluOpType
+ACT = mybir.ActivationFunctionType
+
+S, D, L, H, DH, R = 512, 2048, 512, 16, 128, 64
+HALF = R // 2
+P = 128
+MT = S // P
+G = D // 512
+NB = 512
+HB = NB // DH
+FLOPS = 2 * S * (D * L + 2 * L * 1024 + 2 * D * 1024)
+
+TWO_PI = 2.0 * math.pi
+TWO_PI_HI = 6.28125
+TWO_PI_LO = TWO_PI - TWO_PI_HI
+
+
+def tile_multiheadlatentattention_pa_w8_kernel(
+    tc, x_bytes, x_scale,
+    wc_words, wc_scales, wqd_words, wqd_scales, wkd_words, wkd_scales,
+    wqr_words, wqr_scales, wkr_words, wkr_scales,
+    out_0, out_1,
+):
+    nc = tc.nc
+    with ExitStack() as ctx:
+        keep = ctx.enter_context(tc.tile_pool(name="keep", bufs=1))
+        work = ctx.enter_context(tc.tile_pool(name="work", bufs=4))
+        psum = ctx.enter_context(tc.psum_pool(name="psum", bufs=2))
+        ctx.enter_context(tc.manual_schedule())
+
+        x8 = [keep.tile([P, D], U8, name="x8_%d" % m) for m in range(MT)]
+        xb = [keep.tile([P, D], BF16, name="xb_%d" % m, align_bytes=64) for m in range(MT)]
+        xq = [keep.tile([P, G, P], U32, name="xq_%d" % m, align_bytes=64) for m in range(MT)]
+        xs = [keep.tile([P, G, P], U8, name="xs_%d" % m, align_bytes=64) for m in range(MT)]
+        xsc = keep.tile([P, G, 4], F32, name="xsc")
+        wc = keep.tile([P, G, L], U32, name="wc", align_bytes=64)
+        wcs = keep.tile([P, L], U8, name="wcs", align_bytes=64)
+        wr = [keep.tile([P, G, 1024], U32, name="wr_%d" % t, align_bytes=64) for t in range(2)]
+        wrs = [keep.tile([P, 1024], U8, name="wrs_%d" % t, align_bytes=64) for t in range(2)]
+        wd = [keep.tile([P, 1024], U32, name="wd_%d" % t, align_bytes=64) for t in range(2)]
+        wds = keep.tile([P, 1024], U8, name="wds", align_bytes=64)
+        ident = keep.tile([P, P], F32, name="ident")
+        warm = keep.tile([P, 1], F32, name="warm")
+        ang = keep.tile([P, MT, HALF], F32, name="ang")
+        turns = keep.tile([P, MT * HALF], I32, name="turns")
+        red = keep.tile([P, MT * HALF], F32, name="red")
+        arg = keep.tile([P, 2, MT * HALF], F32, name="arg")
+        sn = keep.tile([P, 2, MT * HALF], F32, name="sn")
+        sq = keep.tile([P, 2, MT * HALF], F32, name="sq")
+        tab = keep.tile([P, MT, 2, R], F32, name="tab")
+
+        def load_scales(dst, src, base, groups):
+            rows = 4 * groups
+            for q in range(4):
+                nc.sync.dma_start(
+                    out=dst[32 * q + base : 32 * q + base + rows, :].bitcast(I32),
+                    in_=src[:, 4 * q : 4 * q + 4, :].bitcast(I32),
+                )
+
+        def load_x(m):
+            nc.sync.dma_start(out=x8[m][:], in_=x_bytes[0, m * P : (m + 1) * P, :])
+
+        nc.vector.memset(warm[:], 0.0)
+        for t in (wcs, wrs[0], wds, wrs[1]):
+            nc.vector.memset(t[:].bitcast(I32), 0)
+
+        load_x(0)
+        nc.sync.dma_start(out=xsc[:], in_=x_scale.rearrange("a b (g p t) -> p (a b g) t", g=G, t=4))
+        load_scales(wcs, wc_scales, 0, G)
+        load_x(1)
+        for g in range(0, G, 2):
+            nc.sync.dma_start(
+                out=wc[:, g : g + 2, :].bitcast(I32),
+                in_=wc_words[g : g + 2].rearrange("g p n t -> p g (n t)").bitcast(I32),
+            )
+        load_scales(wrs[0], wqr_scales, 0, G)
+        for g in range(G):
+            nc.sync.dma_start(
+                out=wr[0][:, g, :].bitcast(I32), in_=wqr_words[g].rearrange("p n t -> p (n t)").bitcast(I32)
+            )
+        load_x(2)
+        load_x(3)
+        load_scales(wds, wqd_scales, 0, 1)
+        load_scales(wds, wkd_scales, 4, 1)
+        for t, w in enumerate((wqd_words, wkd_words)):
+            nc.sync.dma_start(out=wd[t][:].bitcast(I32), in_=w[0].rearrange("p n t -> p (n t)").bitcast(I32))
+        load_scales(wrs[1], wkr_scales, 0, G)
+        for g in range(G):
+            nc.sync.dma_start(
+                out=wr[1][:, g, :].bitcast(I32), in_=wkr_words[g].rearrange("p n t -> p (n t)").bitcast(I32)
+            )
+
+        nc.scalar.activation(out=warm[:], in_=warm[:], func=ACT.Sin)
+        make_identity(nc, ident[:])
+        nc.gpsimd.iota(
+            ang[:, :, 0:1], pattern=[[P, MT], [1, 1]], base=0, channel_multiplier=1,
+            allow_small_or_imprecise_dtypes=True,
+        )
+        w = 1
+        while w < HALF:
+            nc.vector.tensor_scalar(
+                out=ang[:, :, w : 2 * w], in0=ang[:, :, 0:w], scalar1=10000.0 ** (-2.0 * w / R), scalar2=None, op0=ALU.mult
+            )
+            w *= 2
+        angf = ang[:].rearrange("p m i -> p (m i)")
+
+        def table_part_1():
+            nc.vector.tensor_scalar(out=turns[:], in0=angf, scalar1=1.0 / TWO_PI, scalar2=None, op0=ALU.mult)
+
+        def table_part_2():
+            nc.vector.scalar_tensor_tensor(out=red[:], in0=turns[:], scalar=-TWO_PI_HI, in1=angf, op0=ALU.mult, op1=ALU.add)
+
+        def table_part_3():
+            nc.vector.scalar_tensor_tensor(out=arg[:, 0, :], in0=turns[:], scalar=-TWO_PI_LO, in1=red[:], op0=ALU.mult, op1=ALU.add)
+
+        def table_part_4():
+            nc.vector.tensor_scalar(out=arg[:, 1, :], in0=arg[:, 0, :], scalar1=-0.5 * math.pi, scalar2=None, op0=ALU.add)
+
+        def table_part_5():
+            nc.scalar.activation(
+                out=sn[:].rearrange("p a i -> p (a i)"), in_=arg[:].rearrange("p a i -> p (a i)"), func=ACT.Sin, scale=0.5
+            )
+            nc.gpsimd.tensor_tensor(out=sq[:], in0=sn[:], in1=sn[:], op=ALU.mult)
+            cos2 = sq[:, 0, :].rearrange("p (m i) -> p m i", m=MT)
+            sin2 = sq[:, 1, :].rearrange("p (m i) -> p m i", m=MT)
+            for lo, src, k in ((0, cos2, 0), (HALF, cos2, 0)):
+                nc.gpsimd.tensor_scalar(out=tab[:, :, k, lo : lo + HALF], in0=src, scalar1=-2.0, scalar2=1.0, op0=ALU.mult, op1=ALU.add)
+            nc.gpsimd.tensor_scalar(out=tab[:, :, 1, 0:HALF], in0=sin2, scalar1=-2.0, scalar2=1.0, op0=ALU.mult, op1=ALU.add)
+            nc.gpsimd.tensor_scalar(out=tab[:, :, 1, HALF:R], in0=sin2, scalar1=2.0, scalar2=-1.0, op0=ALU.mult, op1=ALU.add)
+
+        def cast(m, engine, lo, hi):
+            if engine == "v":
+                nc.vector.tensor_copy(out=xb[m][:, lo:hi], in_=x8[m][:, lo:hi].bitcast(FP8))
+            else:
+                nc.scalar.copy(out=xb[m][:, lo:hi], in_=x8[m][:, lo:hi].bitcast(FP8))
+
+        xt = {}
+
+        def turn(m, pair):
+            bank = psum.tile([P, 2, 2, P], F32, name="xt", tag="xt", bufs=2)
+            words = xb[m][:].bitcast(F32)
+            for i in range(2):
+                g = 2 * pair + i
+                for u in range(2):
+                    nc.tensor.transpose(bank[:, i, u, :], words[:, 256 * g + u : 256 * (g + 1) : 2], ident[:])
+            xt[m, pair] = bank
+
+        gx = {}
+
+        def scale(m, g):
+            t = work.tile([P, P, 4], BF16, name="gx", tag="gx", bufs=4, align_bytes=64)
+            bank = xt[m, g // 2]
+            nc.vector.tensor_tensor(
+                out=t[:].rearrange("p r (u e) -> p r u e", u=2),
+                in0=bank[:, g % 2].rearrange("p u r -> p (u r)").bitcast(BF16).rearrange("p (u r e) -> p r u e", u=2, e=2),
+                in1=xsc[:, g, :].rearrange("p (u e) -> p u e", u=2).unsqueeze(1).to_broadcast([P, P, 2, 2]),
+                op=ALU.mult,
+            )
+            gx[m, g] = t
+
+        def quant(m, g):
+            nc.vector.quantize_mx(
+                out=xq[m][:, g, :].bitcast(FP8X4), scales=xs[m][:, g, :], in_=gx[m, g][:].rearrange("p r j -> p (r j)")
+            )
+
+        cbank, cb, ctb, cg, cq, cs = {}, {}, {}, {}, {}, {}
+
+        def latent(m):
+            b = psum.tile([P, L], F32, name="cc", tag="cc", bufs=2)
+            for g in range(G):
+                nc.tensor.matmul_mx(
+                    out=b[:], lhsT=xq[m][:, g, :].bitcast(FP8X4), lhsT_scale=xs[m][:, g, :],
+                    rhs=wc[:, g, :].bitcast(FP8X4), rhs_scale=wcs[4 * g : P, :],
+                    start=(g == 0), stop=(g == G - 1),
+                )
+            cbank[m] = b
+
+        def latent_out(m):
+            t = work.tile([P, L], BF16, name="cb", tag="cb", bufs=2, align_bytes=64)
+            nc.scalar.copy(
+                out=t[:].rearrange("p (u c e) -> p u c e", u=2, e=2),
+                in_=cbank[m][:].rearrange("p (c u e) -> p u c e", u=2, e=2),
+            )
+            cb[m] = t
+
+        def latent_turn(m):
+            b = psum.tile([P, 2, P], F32, name="cc", tag="cc", bufs=2)
+            words = cb[m][:].bitcast(F32)
+            for u in range(2):
+                nc.tensor.transpose(b[:, u, :], words[:, u * P : (u + 1) * P], ident[:])
+            t = work.tile([P, P, 4], BF16, name="cg", tag="cg", bufs=2, align_bytes=64)
+            nc.scalar.copy(
+                out=t[:].rearrange("p r j -> p (r j)").bitcast(F32).rearrange("p (r u) -> p r u", u=2),
+                in_=b[:].rearrange("p u r -> p r u"),
+            )
+            cg[m] = t
+
+        def latent_quant(m):
+            cq[m] = work.tile([P, P], U32, name="cq", tag="cq", bufs=4, align_bytes=64)
+            cs[m] = work.tile([P, P], U8, name="cs", tag="cs", bufs=4, align_bytes=64)
+            nc.vector.quantize_mx(
+                out=cq[m][:].bitcast(FP8X4), scales=cs[m][:], in_=cg[m][:].rearrange("p r j -> p (r j)")
+            )
+
+        bank, unit = {}, {}
+        outs = [o[0].rearrange("(m p) h d -> m p h d", p=P) for o in (out_0, out_1)]
+
+        def new_bank(key):
+            bank[key] = psum.tile([P, NB], F32, name="ob", tag="ob", bufs=4)
+            return bank[key]
+
+        def rope_pass(key, g):
+            m, t, j = key[1], key[2], key[3]
+            nc.tensor.matmul_mx(
+                out=bank[key][:], lhsT=xq[m][:, g, :].bitcast(FP8X4), lhsT_scale=xs[m][:, g, :],
+                rhs=wr[t][:, g, j * NB : (j + 1) * NB].bitcast(FP8X4), rhs_scale=wrs[t][4 * g : P, j * NB : (j + 1) * NB],
+                start=(g == 0), stop=(g == G - 1),
+            )
+
+        def produce(key):
+            kind, m, t, j = key
+            new_bank(key)
+            if kind == "r":
+                for g in range(G):
+                    rope_pass(key, g)
+            else:
+                nc.tensor.matmul_mx(
+                    out=bank[key][:], lhsT=cq[m][:].bitcast(FP8X4), lhsT_scale=cs[m][:],
+                    rhs=wd[t][:, j * NB : (j + 1) * NB].bitcast(FP8X4), rhs_scale=wds[4 * t : P, j * NB : (j + 1) * NB],
+                    start=True, stop=True,
+                )
+
+        def consume(key):
+            kind, m, t, j = key
+            if j == 0:
+                unit[key[:3]] = (
+                    work.tile([P, 2, 2 * HB, R], F32, name="ab", tag="ab", bufs=4),
+                    work.tile([P, 2 * HB, DH], F32, name="ot", tag="ot", bufs=5),
+                )
+            ab, ot = unit[key[:3]]
+            heads = bank[key][:].rearrange("p (h d) -> p h d", h=HB)
+            hs = slice(HB * j, HB * (j + 1))
+            nc.vector.tensor_tensor(
+                out=ab[:, :, hs, :],
+                in0=heads[:, :, R:DH].unsqueeze(1).to_broadcast([P, 2, HB, R]),
+                in1=tab[:, m].unsqueeze(2).to_broadcast([P, 2, HB, R]),
+                op=ALU.mult,
+            )
+            nc.scalar.copy(out=ot[:, hs, 0:R], in_=heads[:, :, 0:R])
+            if m == MT - 1 and t == 1:
+                part = hs
+            elif j == 1:
+                part = slice(0, 2 * HB)
+            else:
+                return
+            eng = nc.vector if key == ("r", MT - 1, 1, 1) else nc.gpsimd
+            if True:
+                eng.tensor_tensor(out=ot[:, part, R : R + HALF], in0=ab[:, 0, part, 0:HALF], in1=ab[:, 1, part, HALF:R], op=ALU.add)
+                eng.tensor_tensor(out=ot[:, part, R + HALF : DH], in0=ab[:, 0, part, HALF:R], in1=ab[:, 1, part, 0:HALF], op=ALU.add)
+                h0 = 8 * (kind == "r") + part.start
+                nc.sync.dma_start(out=outs[t][m, :, h0 : h0 + part.stop - part.start, :], in_=ot[:, part, :])
+
+        cast(0, "v", 0, 512)
+        cast(0, "s", 512, 1024)
+        cast(0, "v", 1024, 1536)
+        cast(0, "s", 1536, 2048)
+        turn(0, 0)
+        turn(0, 1)
+        scale(0, 0)
+        table_part_1()
+        scale(0, 1)
+        quant(0, 0)
+        table_part_2()
+        scale(0, 2)
+        quant(0, 1)
+        table_part_3()
+        scale(0, 3)
+        quant(0, 2)
+        table_part_4()
+        cast(1, "s", 0, 1024)
+        cast(1, "s", 1024, 2048)
+        turn(1, 0)
+        scale(1, 0)
+        quant(0, 3)
+        table_part_5()
+        latent(0)
+        turn(1, 1)
+        latent_out(0)
+        scale(1, 1)
+        quant(1, 0)
+        cast(2, "s", 0, 1024)
+        cast(2, "s", 1024, 2048)
+        scale(1, 2)
+        quant(1, 1)
+        scale(1, 3)
+        quant(1, 2)
+        b0, b1 = ("r", 0, 0, 0), ("r", 0, 0, 1)
+        new_bank(b0)
+        new_bank(b1)
+        for g in range(G):
+            rope_pass(b0, g)
+            rope_pass(b1, g)
+        latent_turn(0)
+        turn(2, 0)
+        quant(1, 3)
+        latent(1)
+        latent_out(1)
+        scale(2, 0)
+        latent_quant(0)
+
+        def x_steps(m):
+            return [
+                [lambda: turn(m, 1), lambda: scale(m, 1), lambda: quant(m, 0)],
+                [lambda: scale(m, 2), lambda: quant(m, 1)],
+                [lambda: scale(m, 3), lambda: quant(m, 2)],
+                [lambda: quant(m, 3)],
+            ]
+
+        x2, x3 = x_steps(2), x_steps(3)
+        seq = [b0, b1]
+        todo = [
+            (("r", 1, 0, 0), [lambda: latent_turn(1)] + x2[0]),
+            (("r", 1, 0, 1), x2[1] + [lambda: latent_quant(1)]),
+            (("d", 0, 0, 0), x2[2]),
+            (("d", 0, 0, 1), x2[3]),
+            (("r", 2, 0, 0), [lambda: latent(2), lambda: latent_out(2)]),
+            (("d", 0, 1, 0), [lambda: cast(3, "s", 0, 1024)]),
+            (("r", 2, 0, 1), [lambda: cast(3, "s", 1024, 2048)]),
+            (("d", 0, 1, 1), []),
+            (("r", 0, 1, 0), [lambda: latent_turn(2), lambda: turn(3, 0)]),
+            (("d", 1, 0, 0), [lambda: scale(3, 0), lambda: latent_quant(2)]),
+            (("r", 0, 1, 1), x3[0]),
+            (("d", 1, 0, 1), []),
+            (("r", 1, 1, 0), x3[1]),
+            (("d", 1, 1, 0), []),
+            (("r", 1, 1, 1), x3[2]),
+            (("d", 1, 1, 1), x3[3]),
+            (("r", 2, 1, 0), [lambda: latent(3), lambda: latent_out(3)]),
+            (("d", 2, 0, 0), []),
+            (("r", 2, 1, 1), []),
+            (("d", 2, 0, 1), [lambda: latent_turn(3)]),
+            (("r", 3, 0, 0), [lambda: latent_quant(3)]),
+            (("d", 2, 1, 0), []),
+            (("r", 3, 0, 1), []),
+            (("d", 2, 1, 1), []),
+            (("d", 3, 0, 0), []),
+            (("d", 3, 0, 1), []),
+            (("d", 3, 1, 0), []),
+            (("r", 3, 1, 0), []),
+            (("d", 3, 1, 1), []),
+            (("r", 3, 1, 1), []),
+        ]
+        lag = 2
+        for key, before in todo:
+            for step in before:
+                step()
+            produce(key)
+            seq.append(key)
+            consume(seq[len(seq) - 1 - lag])
+        for i in range(lag):
+            key = seq[len(seq) - lag + i]
+            consume(key)

@@ -21,6 +21,8 @@ MT = S // P
 G = D // 512
 NB = 512
 HB = NB // DH
+BUFS = {"xt": 2, "cc": 1, "ob": 5}
+WARM = 6
 FLOPS = 2 * S * (D * L + 2 * L * 1024 + 2 * D * 1024)
 
 TWO_PI = 2.0 * math.pi
@@ -54,6 +56,8 @@ def tile_multiheadlatentattention_pa_w8_kernel(
         wds = keep.tile([P, 1024], U8, name="wds", align_bytes=64)
         ident = keep.tile([P, P], F32, name="ident")
         warm = keep.tile([P, 1], F32, name="warm")
+        dummy = keep.tile([P, 512], BF16, name="dummy")
+        gx = [keep.tile([P, G, P, 4], BF16, name="gx_%d" % m, align_bytes=64) for m in range(MT)]
         ang = keep.tile([P, MT, HALF], F32, name="ang")
         turns = keep.tile([P, MT * HALF], I32, name="turns")
         red = keep.tile([P, MT * HALF], F32, name="red")
@@ -73,12 +77,21 @@ def tile_multiheadlatentattention_pa_w8_kernel(
         def load_x(m):
             nc.sync.dma_start(out=x8[m][:], in_=x_bytes[0, m * P : (m + 1) * P, :])
 
+        nc.scalar.dma_start(out=xsc[:], in_=x_scale.rearrange("a b (g p t) -> p (a b g) t", g=G, t=4))
+        for lo in (0, D // 2):
+            nc.sync.dma_start(out=x8[0][:, lo : lo + D // 2], in_=x_bytes[0, 0:P, lo : lo + D // 2])
+        nc.gpsimd.iota(
+            ang[:, :, 0:1], pattern=[[P, MT], [1, 1]], base=0, channel_multiplier=1,
+            allow_small_or_imprecise_dtypes=True,
+        )
+        make_identity(nc, ident[:])
         nc.vector.memset(warm[:], 0.0)
-        for t in (wcs, wrs[0], wds, wrs[1]):
+        nc.scalar.activation(out=warm[:], in_=warm[:], func=ACT.Sin)
+        for t in (wcs, wrs[0]):
             nc.vector.memset(t[:].bitcast(I32), 0)
-
-        load_x(0)
-        nc.sync.dma_start(out=xsc[:], in_=x_scale.rearrange("a b (g p t) -> p (a b g) t", g=G, t=4))
+        nc.vector.memset(dummy[:], 0.0)
+        for t in (wds, wrs[1]):
+            nc.gpsimd.memset(t[:].bitcast(I32), 0)
         load_scales(wcs, wc_scales, 0, G)
         load_x(1)
         for g in range(0, G, 2):
@@ -87,12 +100,13 @@ def tile_multiheadlatentattention_pa_w8_kernel(
                 in_=wc_words[g : g + 2].rearrange("g p n t -> p g (n t)").bitcast(I32),
             )
         load_scales(wrs[0], wqr_scales, 0, G)
+        load_x(2)
         for g in range(G):
+            if g == 2:
+                load_x(3)
             nc.sync.dma_start(
                 out=wr[0][:, g, :].bitcast(I32), in_=wqr_words[g].rearrange("p n t -> p (n t)").bitcast(I32)
             )
-        load_x(2)
-        load_x(3)
         load_scales(wds, wqd_scales, 0, 1)
         load_scales(wds, wkd_scales, 4, 1)
         for t, w in enumerate((wqd_words, wkd_words)):
@@ -103,12 +117,6 @@ def tile_multiheadlatentattention_pa_w8_kernel(
                 out=wr[1][:, g, :].bitcast(I32), in_=wkr_words[g].rearrange("p n t -> p (n t)").bitcast(I32)
             )
 
-        nc.scalar.activation(out=warm[:], in_=warm[:], func=ACT.Sin)
-        make_identity(nc, ident[:])
-        nc.gpsimd.iota(
-            ang[:, :, 0:1], pattern=[[P, MT], [1, 1]], base=0, channel_multiplier=1,
-            allow_small_or_imprecise_dtypes=True,
-        )
         w = 1
         while w < HALF:
             nc.vector.tensor_scalar(
@@ -149,8 +157,8 @@ def tile_multiheadlatentattention_pa_w8_kernel(
 
         xt = {}
 
-        def turn(m, pair):
-            bank = psum.tile([P, 2, 2, P], F32, name="xt", tag="xt", bufs=2)
+        def turn(m, pair, tag="xt"):
+            bank = psum.tile([P, 2, 2, P], F32, name="xt", tag=tag, bufs=BUFS[tag])
             words = xb[m][:].bitcast(F32)
             for i in range(2):
                 g = 2 * pair + i
@@ -158,28 +166,25 @@ def tile_multiheadlatentattention_pa_w8_kernel(
                     nc.tensor.transpose(bank[:, i, u, :], words[:, 256 * g + u : 256 * (g + 1) : 2], ident[:])
             xt[m, pair] = bank
 
-        gx = {}
-
         def scale(m, g):
-            t = work.tile([P, P, 4], BF16, name="gx", tag="gx", bufs=4, align_bytes=64)
-            bank = xt[m, g // 2]
             nc.vector.tensor_tensor(
-                out=t[:].rearrange("p r (u e) -> p r u e", u=2),
-                in0=bank[:, g % 2].rearrange("p u r -> p (u r)").bitcast(BF16).rearrange("p (u r e) -> p r u e", u=2, e=2),
+                out=gx[m][:, g].rearrange("p r (u e) -> p r u e", u=2),
+                in0=xt[m, g // 2][:, g % 2].rearrange("p u r -> p (u r)").bitcast(BF16).rearrange("p (u r e) -> p r u e", u=2, e=2),
                 in1=xsc[:, g, :].rearrange("p (u e) -> p u e", u=2).unsqueeze(1).to_broadcast([P, P, 2, 2]),
                 op=ALU.mult,
             )
-            gx[m, g] = t
 
-        def quant(m, g):
+        def quant(m, lo, hi):
             nc.vector.quantize_mx(
-                out=xq[m][:, g, :].bitcast(FP8X4), scales=xs[m][:, g, :], in_=gx[m, g][:].rearrange("p r j -> p (r j)")
+                out=xq[m][:, lo:hi, :].rearrange("p g r -> p (g r)").bitcast(FP8X4),
+                scales=xs[m][:, lo:hi, :].rearrange("p g r -> p (g r)"),
+                in_=gx[m][:, lo:hi].rearrange("p g r j -> p (g r j)"),
             )
 
         cbank, cb, ctb, cg, cq, cs = {}, {}, {}, {}, {}, {}
 
         def latent(m):
-            b = psum.tile([P, L], F32, name="cc", tag="cc", bufs=2)
+            b = psum.tile([P, L], F32, name="cc", tag="cc", bufs=BUFS["cc"])
             for g in range(G):
                 nc.tensor.matmul_mx(
                     out=b[:], lhsT=xq[m][:, g, :].bitcast(FP8X4), lhsT_scale=xs[m][:, g, :],
@@ -197,7 +202,7 @@ def tile_multiheadlatentattention_pa_w8_kernel(
             cb[m] = t
 
         def latent_turn(m):
-            b = psum.tile([P, 2, P], F32, name="cc", tag="cc", bufs=2)
+            b = psum.tile([P, 2, P], F32, name="cc", tag="cc", bufs=BUFS["cc"])
             words = cb[m][:].bitcast(F32)
             for u in range(2):
                 nc.tensor.transpose(b[:, u, :], words[:, u * P : (u + 1) * P], ident[:])
@@ -219,7 +224,7 @@ def tile_multiheadlatentattention_pa_w8_kernel(
         outs = [o[0].rearrange("(m p) h d -> m p h d", p=P) for o in (out_0, out_1)]
 
         def new_bank(key):
-            bank[key] = psum.tile([P, NB], F32, name="ob", tag="ob", bufs=4)
+            bank[key] = psum.tile([P, NB], F32, name="ob", tag="ob", bufs=BUFS["ob"])
             return bank[key]
 
         def rope_pass(key, g):
@@ -260,7 +265,7 @@ def tile_multiheadlatentattention_pa_w8_kernel(
                 op=ALU.mult,
             )
             nc.scalar.copy(out=ot[:, hs, 0:R], in_=heads[:, :, 0:R])
-            if m == MT - 1 and t == 1:
+            if m == MT - 1 and t == 1 and kind == "r":
                 part = hs
             elif j == 1:
                 part = slice(0, 2 * HB)
@@ -273,96 +278,97 @@ def tile_multiheadlatentattention_pa_w8_kernel(
                 h0 = 8 * (kind == "r") + part.start
                 nc.sync.dma_start(out=outs[t][m, :, h0 : h0 + part.stop - part.start, :], in_=ot[:, part, :])
 
+        wb = psum.tile([P, 512], F32, name="wb", tag="cc", bufs=BUFS["cc"])
+        for w in range(WARM):
+            nc.tensor.matmul(wb[:], lhsT=dummy[:, 0:P], rhs=dummy[:], start=True, stop=True)
+        table_part_1()
+        table_part_2()
+        table_part_3()
+        table_part_4()
         cast(0, "v", 0, 512)
         cast(0, "s", 512, 1024)
         cast(0, "v", 1024, 1536)
         cast(0, "s", 1536, 2048)
+        table_part_5()
         turn(0, 0)
         turn(0, 1)
         scale(0, 0)
-        table_part_1()
         scale(0, 1)
-        quant(0, 0)
-        table_part_2()
+        quant(0, 0, 1)
         scale(0, 2)
-        quant(0, 1)
-        table_part_3()
-        scale(0, 3)
-        quant(0, 2)
-        table_part_4()
+        quant(0, 1, 2)
         cast(1, "s", 0, 1024)
         cast(1, "s", 1024, 2048)
-        turn(1, 0)
-        scale(1, 0)
-        quant(0, 3)
-        table_part_5()
-        latent(0)
-        turn(1, 1)
-        latent_out(0)
-        scale(1, 1)
-        quant(1, 0)
         cast(2, "s", 0, 1024)
         cast(2, "s", 1024, 2048)
+        turn(1, 0)
+        turn(1, 1, "ob")
+        scale(0, 3)
+        quant(0, 2, 3)
+        scale(1, 0)
+        quant(0, 3, 4)
+        latent(0)
+        latent_out(0)
+        turn(2, 0)
+        scale(1, 1)
         scale(1, 2)
-        quant(1, 1)
+        quant(1, 0, 2)
         scale(1, 3)
-        quant(1, 2)
         b0, b1 = ("r", 0, 0, 0), ("r", 0, 0, 1)
         new_bank(b0)
         new_bank(b1)
-        for g in range(G):
+        for g in (0, 1):
             rope_pass(b0, g)
             rope_pass(b1, g)
         latent_turn(0)
-        turn(2, 0)
-        quant(1, 3)
+        turn(2, 1)
+        scale(2, 0)
+        quant(1, 2, 4)
         latent(1)
         latent_out(1)
-        scale(2, 0)
+        for g in (2, 3):
+            rope_pass(b0, g)
+            rope_pass(b1, g)
+        scale(2, 1)
         latent_quant(0)
-
-        def x_steps(m):
-            return [
-                [lambda: turn(m, 1), lambda: scale(m, 1), lambda: quant(m, 0)],
-                [lambda: scale(m, 2), lambda: quant(m, 1)],
-                [lambda: scale(m, 3), lambda: quant(m, 2)],
-                [lambda: quant(m, 3)],
-            ]
-
-        x2, x3 = x_steps(2), x_steps(3)
-        seq = [b0, b1]
+        scale(2, 2)
+        scale(2, 3)
+        cast(3, "s", 0, 1024)
+        cast(3, "s", 1024, 2048)
+        latent_turn(1)
         todo = [
-            (("r", 1, 0, 0), [lambda: latent_turn(1)] + x2[0]),
-            (("r", 1, 0, 1), x2[1] + [lambda: latent_quant(1)]),
-            (("d", 0, 0, 0), x2[2]),
-            (("d", 0, 0, 1), x2[3]),
-            (("r", 2, 0, 0), [lambda: latent(2), lambda: latent_out(2)]),
-            (("d", 0, 1, 0), [lambda: cast(3, "s", 0, 1024)]),
-            (("r", 2, 0, 1), [lambda: cast(3, "s", 1024, 2048)]),
-            (("d", 0, 1, 1), []),
-            (("r", 0, 1, 0), [lambda: latent_turn(2), lambda: turn(3, 0)]),
-            (("d", 1, 0, 0), [lambda: scale(3, 0), lambda: latent_quant(2)]),
-            (("r", 0, 1, 1), x3[0]),
-            (("d", 1, 0, 1), []),
-            (("r", 1, 1, 0), x3[1]),
-            (("d", 1, 1, 0), []),
-            (("r", 1, 1, 1), x3[2]),
-            (("d", 1, 1, 1), x3[3]),
-            (("r", 2, 1, 0), [lambda: latent(3), lambda: latent_out(3)]),
+            (("r", 1, 0, 0), [lambda: quant(2, 0, 4), lambda: turn(3, 0)]),
+            (("r", 1, 0, 1), [lambda: turn(3, 1), lambda: latent_quant(1)]),
+            (("d", 0, 0, 0), [lambda: scale(3, 0), lambda: latent(2), lambda: latent_out(2)]),
+            (("r", 2, 0, 0), [lambda: scale(3, 1)]),
+            (("d", 0, 0, 1), [lambda: latent_turn(2)]),
+            (("r", 2, 0, 1), [lambda: scale(3, 2)]),
+            (("d", 0, 1, 0), [lambda: latent_quant(2)]),
+            (("d", 0, 1, 1), [lambda: scale(3, 3)]),
+            (("r", 0, 1, 0), []),
+            (("d", 1, 0, 0), [lambda: quant(3, 0, 4)]),
+            (("r", 0, 1, 1), []),
+            (("d", 1, 0, 1), [lambda: latent(3), lambda: latent_out(3)]),
+            (("r", 1, 1, 0), []),
+            (("d", 1, 1, 0), [lambda: latent_turn(3)]),
+            (("r", 1, 1, 1), []),
+            (("d", 1, 1, 1), [lambda: latent_quant(3)]),
+            (("r", 2, 1, 0), []),
             (("d", 2, 0, 0), []),
+            (("d", 2, 0, 1), []),
             (("r", 2, 1, 1), []),
-            (("d", 2, 0, 1), [lambda: latent_turn(3)]),
-            (("r", 3, 0, 0), [lambda: latent_quant(3)]),
             (("d", 2, 1, 0), []),
-            (("r", 3, 0, 1), []),
             (("d", 2, 1, 1), []),
+            (("r", 3, 0, 0), []),
             (("d", 3, 0, 0), []),
             (("d", 3, 0, 1), []),
+            (("r", 3, 0, 1), []),
             (("d", 3, 1, 0), []),
-            (("r", 3, 1, 0), []),
             (("d", 3, 1, 1), []),
+            (("r", 3, 1, 0), []),
             (("r", 3, 1, 1), []),
         ]
+        seq = [b0, b1]
         lag = 2
         for key, before in todo:
             for step in before:
@@ -371,5 +377,4 @@ def tile_multiheadlatentattention_pa_w8_kernel(
             seq.append(key)
             consume(seq[len(seq) - 1 - lag])
         for i in range(lag):
-            key = seq[len(seq) - lag + i]
-            consume(key)
+            consume(seq[len(seq) - lag + i])

@@ -22,7 +22,8 @@ G = D // 512
 NB = 512
 HB = NB // DH
 BUFS = {"xt": 2, "cc": 1, "ob": 5}
-WARM = 6
+WARM = 5
+VADDS = {("r", 3, 1), ("d", 3, 1)}
 FLOPS = 2 * S * (D * L + 2 * L * 1024 + 2 * D * 1024)
 
 TWO_PI = 2.0 * math.pi
@@ -44,20 +45,20 @@ def tile_multiheadlatentattention_pa_w8_kernel(
         ctx.enter_context(tc.manual_schedule())
 
         x8 = [keep.tile([P, D], U8, name="x8_%d" % m) for m in range(MT)]
-        xb = [keep.tile([P, D], BF16, name="xb_%d" % m, align_bytes=64) for m in range(MT)]
-        xq = [keep.tile([P, G, P], U32, name="xq_%d" % m, align_bytes=64) for m in range(MT)]
-        xs = [keep.tile([P, G, P], U8, name="xs_%d" % m, align_bytes=64) for m in range(MT)]
+        xb = [keep.tile([P, D], BF16, name="xb_%d" % m, align_bytes=256) for m in range(MT)]
+        xq = [keep.tile([P, G, P], U32, name="xq_%d" % m, align_bytes=256) for m in range(MT)]
+        xs = [keep.tile([P, G, P], U8, name="xs_%d" % m, align_bytes=256) for m in range(MT)]
         xsc = keep.tile([P, G, 4], F32, name="xsc")
-        wc = keep.tile([P, G, L], U32, name="wc", align_bytes=64)
-        wcs = keep.tile([P, L], U8, name="wcs", align_bytes=64)
-        wr = [keep.tile([P, G, 1024], U32, name="wr_%d" % t, align_bytes=64) for t in range(2)]
-        wrs = [keep.tile([P, 1024], U8, name="wrs_%d" % t, align_bytes=64) for t in range(2)]
-        wd = [keep.tile([P, 1024], U32, name="wd_%d" % t, align_bytes=64) for t in range(2)]
-        wds = keep.tile([P, 1024], U8, name="wds", align_bytes=64)
+        wc = keep.tile([P, G, L], U32, name="wc", align_bytes=256)
+        wcs = keep.tile([P, L], U8, name="wcs", align_bytes=256)
+        wr = [keep.tile([P, G, 1024], U32, name="wr_%d" % t, align_bytes=256) for t in range(2)]
+        wrs = [keep.tile([P, 1024], U8, name="wrs_%d" % t, align_bytes=256) for t in range(2)]
+        wd = [keep.tile([P, 1024], U32, name="wd_%d" % t, align_bytes=256) for t in range(2)]
+        wds = keep.tile([P, 1024], U8, name="wds", align_bytes=256)
         ident = keep.tile([P, P], F32, name="ident")
         warm = keep.tile([P, 1], F32, name="warm")
         dummy = keep.tile([P, 512], BF16, name="dummy")
-        gx = [keep.tile([P, G, P, 4], BF16, name="gx_%d" % m, align_bytes=64) for m in range(MT)]
+        gx = [keep.tile([P, G, P, 4], BF16, name="gx_%d" % m, align_bytes=256) for m in range(MT)]
         ang = keep.tile([P, MT, HALF], F32, name="ang")
         turns = keep.tile([P, MT * HALF], I32, name="turns")
         red = keep.tile([P, MT * HALF], F32, name="red")
@@ -92,14 +93,14 @@ def tile_multiheadlatentattention_pa_w8_kernel(
         nc.vector.memset(dummy[:], 0.0)
         for t in (wds, wrs[1]):
             nc.gpsimd.memset(t[:].bitcast(I32), 0)
-        load_scales(wcs, wc_scales, 0, G)
         load_x(1)
+        load_scales(wcs, wc_scales, 0, G)
+        load_scales(wrs[0], wqr_scales, 0, G)
         for g in range(0, G, 2):
             nc.sync.dma_start(
                 out=wc[:, g : g + 2, :].bitcast(I32),
                 in_=wc_words[g : g + 2].rearrange("g p n t -> p g (n t)").bitcast(I32),
             )
-        load_scales(wrs[0], wqr_scales, 0, G)
         load_x(2)
         for g in range(G):
             if g == 2:
@@ -109,9 +110,9 @@ def tile_multiheadlatentattention_pa_w8_kernel(
             )
         load_scales(wds, wqd_scales, 0, 1)
         load_scales(wds, wkd_scales, 4, 1)
+        load_scales(wrs[1], wkr_scales, 0, G)
         for t, w in enumerate((wqd_words, wkd_words)):
             nc.sync.dma_start(out=wd[t][:].bitcast(I32), in_=w[0].rearrange("p n t -> p (n t)").bitcast(I32))
-        load_scales(wrs[1], wkr_scales, 0, G)
         for g in range(G):
             nc.sync.dma_start(
                 out=wr[1][:, g, :].bitcast(I32), in_=wkr_words[g].rearrange("p n t -> p (n t)").bitcast(I32)
@@ -194,7 +195,7 @@ def tile_multiheadlatentattention_pa_w8_kernel(
             cbank[m] = b
 
         def latent_out(m):
-            t = work.tile([P, L], BF16, name="cb", tag="cb", bufs=2, align_bytes=64)
+            t = work.tile([P, L], BF16, name="cb", tag="cb", bufs=2, align_bytes=256)
             nc.scalar.copy(
                 out=t[:].rearrange("p (u c e) -> p u c e", u=2, e=2),
                 in_=cbank[m][:].rearrange("p (c u e) -> p u c e", u=2, e=2),
@@ -206,7 +207,7 @@ def tile_multiheadlatentattention_pa_w8_kernel(
             words = cb[m][:].bitcast(F32)
             for u in range(2):
                 nc.tensor.transpose(b[:, u, :], words[:, u * P : (u + 1) * P], ident[:])
-            t = work.tile([P, P, 4], BF16, name="cg", tag="cg", bufs=2, align_bytes=64)
+            t = work.tile([P, P, 4], BF16, name="cg", tag="cg", bufs=2, align_bytes=256)
             nc.scalar.copy(
                 out=t[:].rearrange("p r j -> p (r j)").bitcast(F32).rearrange("p (r u) -> p r u", u=2),
                 in_=b[:].rearrange("p u r -> p r u"),
@@ -214,13 +215,13 @@ def tile_multiheadlatentattention_pa_w8_kernel(
             cg[m] = t
 
         def latent_quant(m):
-            cq[m] = work.tile([P, P], U32, name="cq", tag="cq", bufs=4, align_bytes=64)
-            cs[m] = work.tile([P, P], U8, name="cs", tag="cs", bufs=4, align_bytes=64)
+            cq[m] = work.tile([P, P], U32, name="cq", tag="cq", bufs=4, align_bytes=256)
+            cs[m] = work.tile([P, P], U8, name="cs", tag="cs", bufs=4, align_bytes=256)
             nc.vector.quantize_mx(
                 out=cq[m][:].bitcast(FP8X4), scales=cs[m][:], in_=cg[m][:].rearrange("p r j -> p (r j)")
             )
 
-        bank, unit = {}, {}
+        bank, unit, pending = {}, {}, []
         outs = [o[0].rearrange("(m p) h d -> m p h d", p=P) for o in (out_0, out_1)]
 
         def new_bank(key):
@@ -228,59 +229,72 @@ def tile_multiheadlatentattention_pa_w8_kernel(
             return bank[key]
 
         def rope_pass(key, g):
-            m, t, j = key[1], key[2], key[3]
+            kind, m, t, h0, nh = key
+            cols = slice(h0 * DH, (h0 + nh) * DH)
             nc.tensor.matmul_mx(
-                out=bank[key][:], lhsT=xq[m][:, g, :].bitcast(FP8X4), lhsT_scale=xs[m][:, g, :],
-                rhs=wr[t][:, g, j * NB : (j + 1) * NB].bitcast(FP8X4), rhs_scale=wrs[t][4 * g : P, j * NB : (j + 1) * NB],
+                out=bank[key][:, 0 : nh * DH], lhsT=xq[m][:, g, :].bitcast(FP8X4), lhsT_scale=xs[m][:, g, :],
+                rhs=wr[t][:, g, cols].bitcast(FP8X4), rhs_scale=wrs[t][4 * g : P, cols],
                 start=(g == 0), stop=(g == G - 1),
             )
 
         def produce(key):
-            kind, m, t, j = key
+            kind, m, t, h0, nh = key
             new_bank(key)
             if kind == "r":
                 for g in range(G):
                     rope_pass(key, g)
             else:
+                cols = slice(h0 * DH, (h0 + nh) * DH)
                 nc.tensor.matmul_mx(
                     out=bank[key][:], lhsT=cq[m][:].bitcast(FP8X4), lhsT_scale=cs[m][:],
-                    rhs=wd[t][:, j * NB : (j + 1) * NB].bitcast(FP8X4), rhs_scale=wds[4 * t : P, j * NB : (j + 1) * NB],
+                    rhs=wd[t][:, cols].bitcast(FP8X4), rhs_scale=wds[4 * t : P, cols],
                     start=True, stop=True,
                 )
 
         def consume(key):
-            kind, m, t, j = key
-            if j == 0:
+            kind, m, t, h0, nh = key
+            if key[:3] not in unit:
                 unit[key[:3]] = (
                     work.tile([P, 2, 2 * HB, R], F32, name="ab", tag="ab", bufs=4),
-                    work.tile([P, 2 * HB, DH], F32, name="ot", tag="ot", bufs=5),
+                    work.tile([P, 2 * HB, DH], F32, name="ot", tag="ot", bufs=6),
                 )
             ab, ot = unit[key[:3]]
-            heads = bank[key][:].rearrange("p (h d) -> p h d", h=HB)
-            hs = slice(HB * j, HB * (j + 1))
+            heads = bank[key][:, 0 : nh * DH].rearrange("p (h d) -> p h d", h=nh)
+            hs = slice(h0, h0 + nh)
             nc.vector.tensor_tensor(
                 out=ab[:, :, hs, :],
-                in0=heads[:, :, R:DH].unsqueeze(1).to_broadcast([P, 2, HB, R]),
-                in1=tab[:, m].unsqueeze(2).to_broadcast([P, 2, HB, R]),
+                in0=heads[:, :, R:DH].unsqueeze(1).to_broadcast([P, 2, nh, R]),
+                in1=tab[:, m].unsqueeze(2).to_broadcast([P, 2, nh, R]),
                 op=ALU.mult,
             )
             nc.scalar.copy(out=ot[:, hs, 0:R], in_=heads[:, :, 0:R])
-            if m == MT - 1 and t == 1 and kind == "r":
+            while pending:
+                finish(*pending.pop())
+            if key[:3] == ("r", MT - 1, 1):
                 part = hs
-            elif j == 1:
+            elif h0 == HB:
                 part = slice(0, 2 * HB)
             else:
                 return
-            eng = nc.vector if key == ("r", MT - 1, 1, 1) else nc.gpsimd
-            if True:
-                eng.tensor_tensor(out=ot[:, part, R : R + HALF], in0=ab[:, 0, part, 0:HALF], in1=ab[:, 1, part, HALF:R], op=ALU.add)
-                eng.tensor_tensor(out=ot[:, part, R + HALF : DH], in0=ab[:, 0, part, HALF:R], in1=ab[:, 1, part, 0:HALF], op=ALU.add)
-                h0 = 8 * (kind == "r") + part.start
-                nc.sync.dma_start(out=outs[t][m, :, h0 : h0 + part.stop - part.start, :], in_=ot[:, part, :])
+            if key[:3] in VADDS:
+                pending.append((nc.vector, key, part))
+            else:
+                finish(nc.gpsimd, key, part)
 
-        wb = psum.tile([P, 512], F32, name="wb", tag="cc", bufs=BUFS["cc"])
-        for w in range(WARM):
-            nc.tensor.matmul(wb[:], lhsT=dummy[:, 0:P], rhs=dummy[:], start=True, stop=True)
+        def finish(eng, key, part):
+            kind, m, t = key[:3]
+            ab, ot = unit[key[:3]]
+            eng.tensor_tensor(out=ot[:, part, R : R + HALF], in0=ab[:, 0, part, 0:HALF], in1=ab[:, 1, part, HALF:R], op=ALU.add)
+            eng.tensor_tensor(out=ot[:, part, R + HALF : DH], in0=ab[:, 0, part, HALF:R], in1=ab[:, 1, part, 0:HALF], op=ALU.add)
+            f0 = 8 * (kind == "r") + part.start
+            nc.sync.dma_start(out=outs[t][m, :, f0 : f0 + part.stop - part.start, :], in_=ot[:, part, :])
+
+        def warm_up(n):
+            wb = psum.tile([P, 512], F32, name="wb", tag="cc", bufs=BUFS["cc"])
+            for w in range(n):
+                nc.tensor.matmul(wb[:], lhsT=dummy[:, 0:P], rhs=dummy[:], start=True, stop=True)
+
+        warm_up(WARM)
         table_part_1()
         table_part_2()
         table_part_3()
@@ -314,7 +328,7 @@ def tile_multiheadlatentattention_pa_w8_kernel(
         scale(1, 2)
         quant(1, 0, 2)
         scale(1, 3)
-        b0, b1 = ("r", 0, 0, 0), ("r", 0, 0, 1)
+        b0, b1 = ("r", 0, 0, 0, HB), ("r", 0, 0, HB, HB)
         new_bank(b0)
         new_bank(b1)
         for g in (0, 1):
@@ -335,46 +349,54 @@ def tile_multiheadlatentattention_pa_w8_kernel(
         scale(2, 3)
         cast(3, "s", 0, 1024)
         cast(3, "s", 1024, 2048)
-        latent_turn(1)
         todo = [
-            (("r", 1, 0, 0), [lambda: quant(2, 0, 4), lambda: turn(3, 0)]),
-            (("r", 1, 0, 1), [lambda: turn(3, 1), lambda: latent_quant(1)]),
-            (("d", 0, 0, 0), [lambda: scale(3, 0), lambda: latent(2), lambda: latent_out(2)]),
-            (("r", 2, 0, 0), [lambda: scale(3, 1)]),
-            (("d", 0, 0, 1), [lambda: latent_turn(2)]),
-            (("r", 2, 0, 1), [lambda: scale(3, 2)]),
-            (("d", 0, 1, 0), [lambda: latent_quant(2)]),
-            (("d", 0, 1, 1), [lambda: scale(3, 3)]),
-            (("r", 0, 1, 0), []),
-            (("d", 1, 0, 0), [lambda: quant(3, 0, 4)]),
-            (("r", 0, 1, 1), []),
-            (("d", 1, 0, 1), [lambda: latent(3), lambda: latent_out(3)]),
-            (("r", 1, 1, 0), []),
-            (("d", 1, 1, 0), [lambda: latent_turn(3)]),
-            (("r", 1, 1, 1), []),
-            (("d", 1, 1, 1), [lambda: latent_quant(3)]),
-            (("r", 2, 1, 0), []),
-            (("d", 2, 0, 0), []),
-            (("d", 2, 0, 1), []),
-            (("r", 2, 1, 1), []),
-            (("d", 2, 1, 0), []),
-            (("d", 2, 1, 1), []),
-            (("r", 3, 0, 0), []),
-            (("d", 3, 0, 0), []),
-            (("d", 3, 0, 1), []),
-            (("r", 3, 0, 1), []),
-            (("d", 3, 1, 0), []),
-            (("d", 3, 1, 1), []),
-            (("r", 3, 1, 0), []),
-            (("r", 3, 1, 1), []),
+            ("r10", [lambda: quant(2, 0, 4)]),
+            ("r10", [lambda: latent_turn(1), lambda: turn(3, 0), lambda: turn(3, 1), lambda: latent_quant(1)]),
+            ("d00", [lambda: scale(3, 0), lambda: latent(2), lambda: latent_out(2)]),
+            ("r20", [lambda: scale(3, 1)]),
+            ("d00", [lambda: latent_turn(2)]),
+            ("r20", [lambda: scale(3, 2)]),
+            ("d01", [lambda: latent_quant(2)]),
+            ("d01", [lambda: scale(3, 3)]),
+            ("r01", []),
+            ("d10", [lambda: quant(3, 0, 4)]),
+            ("r01", []),
+            ("d10", [lambda: latent(3), lambda: latent_out(3)]),
+            ("r11", []),
+            ("d11", [lambda: latent_turn(3)]),
+            ("r11", []),
+            ("d11", [lambda: latent_quant(3)]),
+            ("r21", []),
+            ("d20", []),
+            ("d20", []),
+            ("r21", []),
+            ("d21", []),
+            ("d21", []),
+            ("r30", []),
+            ("d30", []),
+            ("d30", []),
+            ("r30", []),
+            ("d31", []),
+            ("d31", []),
+            ("r31", []),
+            ("r31a", []),
+            ("r31b", []),
         ]
         seq = [b0, b1]
+        seen = {}
         lag = 2
-        for key, before in todo:
+        for code, before in todo:
             for step in before:
                 step()
+            unit_key = (code[0], int(code[1]), int(code[2]))
+            h0 = seen.setdefault(unit_key, 0)
+            nh = 2 if len(code) > 3 else HB
+            seen[unit_key] = h0 + nh
+            key = unit_key + (h0, nh)
             produce(key)
             seq.append(key)
             consume(seq[len(seq) - 1 - lag])
         for i in range(lag):
             consume(seq[len(seq) - lag + i])
+        while pending:
+            finish(*pending.pop())

import math
from contextlib import ExitStack

import concourse.mybir as mybir
from concourse.masks import make_identity

F32 = mybir.dt.float32
BF16 = mybir.dt.bfloat16
I32 = mybir.dt.int32
U32 = mybir.dt.uint32
U8 = mybir.dt.uint8
FP8 = mybir.dt.float8_e4m3fn
FP8X4 = mybir.dt.float8_e4m3fn_x4
ALU = mybir.AluOpType
ACT = mybir.ActivationFunctionType

S, D, L, H, DH, R = 512, 2048, 512, 16, 128, 64
HALF = R // 2
P = 128
MT = S // P
G = D // 512
NB = 512
HB = NB // DH
BUFS = {"xt": 2, "cc": 1, "ob": 5}
WARM = 5
VADDS = {("r", 3, 1), ("d", 3, 1)}
FLOPS = 2 * S * (D * L + 2 * L * 1024 + 2 * D * 1024)

TWO_PI = 2.0 * math.pi
TWO_PI_HI = 6.28125
TWO_PI_LO = TWO_PI - TWO_PI_HI


def tile_multiheadlatentattention_pa_w8_kernel(
    tc, x_bytes, x_scale,
    wc_words, wc_scales, wqd_words, wqd_scales, wkd_words, wkd_scales,
    wqr_words, wqr_scales, wkr_words, wkr_scales,
    out_0, out_1,
):
    nc = tc.nc
    with ExitStack() as ctx:
        keep = ctx.enter_context(tc.tile_pool(name="keep", bufs=1))
        work = ctx.enter_context(tc.tile_pool(name="work", bufs=4))
        psum = ctx.enter_context(tc.psum_pool(name="psum", bufs=2))
        ctx.enter_context(tc.manual_schedule())

        x8 = [keep.tile([P, D], U8, name="x8_%d" % m) for m in range(MT)]
        xb = [keep.tile([P, D], BF16, name="xb_%d" % m, align_bytes=256) for m in range(MT)]
        xq = [keep.tile([P, G, P], U32, name="xq_%d" % m, align_bytes=256) for m in range(MT)]
        xs = [keep.tile([P, G, P], U8, name="xs_%d" % m, align_bytes=256) for m in range(MT)]
        xsc = keep.tile([P, G, 4], F32, name="xsc")
        wc = keep.tile([P, G, L], U32, name="wc", align_bytes=256)
        wcs = keep.tile([P, L], U8, name="wcs", align_bytes=256)
        wr = [keep.tile([P, G, 1024], U32, name="wr_%d" % t, align_bytes=256) for t in range(2)]
        wrs = [keep.tile([P, 1024], U8, name="wrs_%d" % t, align_bytes=256) for t in range(2)]
        wd = [keep.tile([P, 1024], U32, name="wd_%d" % t, align_bytes=256) for t in range(2)]
        wds = keep.tile([P, 1024], U8, name="wds", align_bytes=256)
        ident = keep.tile([P, P], F32, name="ident")
        warm = keep.tile([P, 1], F32, name="warm")
        dummy = keep.tile([P, 512], BF16, name="dummy")
        gx = [keep.tile([P, G, P, 4], BF16, name="gx_%d" % m, align_bytes=256) for m in range(MT)]
        ang = keep.tile([P, MT, HALF], F32, name="ang")
        turns = keep.tile([P, MT * HALF], I32, name="turns")
        red = keep.tile([P, MT * HALF], F32, name="red")
        arg = keep.tile([P, 2, MT * HALF], F32, name="arg")
        sn = keep.tile([P, 2, MT * HALF], F32, name="sn")
        sq = keep.tile([P, 2, MT * HALF], F32, name="sq")
        tab = keep.tile([P, MT, 2, R], F32, name="tab")

        def load_scales(dst, src, base, groups):
            rows = 4 * groups
            for q in range(4):
                nc.sync.dma_start(
                    out=dst[32 * q + base : 32 * q + base + rows, :].bitcast(I32),
                    in_=src[:, 4 * q : 4 * q + 4, :].bitcast(I32),
                )

        def load_x(m):
            nc.sync.dma_start(out=x8[m][:], in_=x_bytes[0, m * P : (m + 1) * P, :])

        nc.scalar.dma_start(out=xsc[:], in_=x_scale.rearrange("a b (g p t) -> p (a b g) t", g=G, t=4))
        for lo in (0, D // 2):
            nc.sync.dma_start(out=x8[0][:, lo : lo + D // 2], in_=x_bytes[0, 0:P, lo : lo + D // 2])
        nc.gpsimd.iota(
            ang[:, :, 0:1], pattern=[[P, MT], [1, 1]], base=0, channel_multiplier=1,
            allow_small_or_imprecise_dtypes=True,
        )
        make_identity(nc, ident[:])
        nc.vector.memset(warm[:], 0.0)
        nc.scalar.activation(out=warm[:], in_=warm[:], func=ACT.Sin)
        for t in (wcs, wrs[0]):
            nc.vector.memset(t[:].bitcast(I32), 0)
        nc.vector.memset(dummy[:], 0.0)
        for t in (wds, wrs[1]):
            nc.gpsimd.memset(t[:].bitcast(I32), 0)
        load_x(1)
        load_scales(wcs, wc_scales, 0, G)
        load_scales(wrs[0], wqr_scales, 0, G)
        for g in range(0, G, 2):
            nc.sync.dma_start(
                out=wc[:, g : g + 2, :].bitcast(I32),
                in_=wc_words[g : g + 2].rearrange("g p n t -> p g (n t)").bitcast(I32),
            )
        load_x(2)
        for g in range(G):
            if g == 2:
                load_x(3)
            nc.sync.dma_start(
                out=wr[0][:, g, :].bitcast(I32), in_=wqr_words[g].rearrange("p n t -> p (n t)").bitcast(I32)
            )
        load_scales(wds, wqd_scales, 0, 1)
        load_scales(wds, wkd_scales, 4, 1)
        load_scales(wrs[1], wkr_scales, 0, G)
        for t, w in enumerate((wqd_words, wkd_words)):
            nc.sync.dma_start(out=wd[t][:].bitcast(I32), in_=w[0].rearrange("p n t -> p (n t)").bitcast(I32))
        for g in range(G):
            nc.sync.dma_start(
                out=wr[1][:, g, :].bitcast(I32), in_=wkr_words[g].rearrange("p n t -> p (n t)").bitcast(I32)
            )

        w = 1
        while w < HALF:
            nc.vector.tensor_scalar(
                out=ang[:, :, w : 2 * w], in0=ang[:, :, 0:w], scalar1=10000.0 ** (-2.0 * w / R), scalar2=None, op0=ALU.mult
            )
            w *= 2
        angf = ang[:].rearrange("p m i -> p (m i)")

        def table_part_1():
            nc.vector.tensor_scalar(out=turns[:], in0=angf, scalar1=1.0 / TWO_PI, scalar2=None, op0=ALU.mult)

        def table_part_2():
            nc.vector.scalar_tensor_tensor(out=red[:], in0=turns[:], scalar=-TWO_PI_HI, in1=angf, op0=ALU.mult, op1=ALU.add)

        def table_part_3():
            nc.vector.scalar_tensor_tensor(out=arg[:, 0, :], in0=turns[:], scalar=-TWO_PI_LO, in1=red[:], op0=ALU.mult, op1=ALU.add)

        def table_part_4():
            nc.vector.tensor_scalar(out=arg[:, 1, :], in0=arg[:, 0, :], scalar1=-0.5 * math.pi, scalar2=None, op0=ALU.add)

        def table_part_5():
            nc.scalar.activation(
                out=sn[:].rearrange("p a i -> p (a i)"), in_=arg[:].rearrange("p a i -> p (a i)"), func=ACT.Sin, scale=0.5
            )
            nc.gpsimd.tensor_tensor(out=sq[:], in0=sn[:], in1=sn[:], op=ALU.mult)
            cos2 = sq[:, 0, :].rearrange("p (m i) -> p m i", m=MT)
            sin2 = sq[:, 1, :].rearrange("p (m i) -> p m i", m=MT)
            for lo, src, k in ((0, cos2, 0), (HALF, cos2, 0)):
                nc.gpsimd.tensor_scalar(out=tab[:, :, k, lo : lo + HALF], in0=src, scalar1=-2.0, scalar2=1.0, op0=ALU.mult, op1=ALU.add)
            nc.gpsimd.tensor_scalar(out=tab[:, :, 1, 0:HALF], in0=sin2, scalar1=-2.0, scalar2=1.0, op0=ALU.mult, op1=ALU.add)
            nc.gpsimd.tensor_scalar(out=tab[:, :, 1, HALF:R], in0=sin2, scalar1=2.0, scalar2=-1.0, op0=ALU.mult, op1=ALU.add)

        def cast(m, engine, lo, hi):
            if engine == "v":
                nc.vector.tensor_copy(out=xb[m][:, lo:hi], in_=x8[m][:, lo:hi].bitcast(FP8))
            else:
                nc.scalar.copy(out=xb[m][:, lo:hi], in_=x8[m][:, lo:hi].bitcast(FP8))

        xt = {}

        def turn(m, pair, tag="xt"):
            bank = psum.tile([P, 2, 2, P], F32, name="xt", tag=tag, bufs=BUFS[tag])
            words = xb[m][:].bitcast(F32)
            for i in range(2):
                g = 2 * pair + i
                for u in range(2):
                    nc.tensor.transpose(bank[:, i, u, :], words[:, 256 * g + u : 256 * (g + 1) : 2], ident[:])
            xt[m, pair] = bank

        def scale(m, g):
            nc.vector.tensor_tensor(
                out=gx[m][:, g].rearrange("p r (u e) -> p r u e", u=2),
                in0=xt[m, g // 2][:, g % 2].rearrange("p u r -> p (u r)").bitcast(BF16).rearrange("p (u r e) -> p r u e", u=2, e=2),
                in1=xsc[:, g, :].rearrange("p (u e) -> p u e", u=2).unsqueeze(1).to_broadcast([P, P, 2, 2]),
                op=ALU.mult,
            )

        def quant(m, lo, hi):
            nc.vector.quantize_mx(
                out=xq[m][:, lo:hi, :].rearrange("p g r -> p (g r)").bitcast(FP8X4),
                scales=xs[m][:, lo:hi, :].rearrange("p g r -> p (g r)"),
                in_=gx[m][:, lo:hi].rearrange("p g r j -> p (g r j)"),
            )

        cbank, cb, ctb, cg, cq, cs = {}, {}, {}, {}, {}, {}

        def latent(m):
            b = psum.tile([P, L], F32, name="cc", tag="cc", bufs=BUFS["cc"])
            for g in range(G):
                nc.tensor.matmul_mx(
                    out=b[:], lhsT=xq[m][:, g, :].bitcast(FP8X4), lhsT_scale=xs[m][:, g, :],
                    rhs=wc[:, g, :].bitcast(FP8X4), rhs_scale=wcs[4 * g : P, :],
                    start=(g == 0), stop=(g == G - 1),
                )
            cbank[m] = b

        def latent_out(m):
            t = work.tile([P, L], BF16, name="cb", tag="cb", bufs=2, align_bytes=256)
            nc.scalar.copy(
                out=t[:].rearrange("p (u c e) -> p u c e", u=2, e=2),
                in_=cbank[m][:].rearrange("p (c u e) -> p u c e", u=2, e=2),
            )
            cb[m] = t

        def latent_turn(m):
            b = psum.tile([P, 2, P], F32, name="cc", tag="cc", bufs=BUFS["cc"])
            words = cb[m][:].bitcast(F32)
            for u in range(2):
                nc.tensor.transpose(b[:, u, :], words[:, u * P : (u + 1) * P], ident[:])
            t = work.tile([P, P, 4], BF16, name="cg", tag="cg", bufs=2, align_bytes=256)
            nc.scalar.copy(
                out=t[:].rearrange("p r j -> p (r j)").bitcast(F32).rearrange("p (r u) -> p r u", u=2),
                in_=b[:].rearrange("p u r -> p r u"),
            )
            cg[m] = t

        def latent_quant(m):
            cq[m] = work.tile([P, P], U32, name="cq", tag="cq", bufs=4, align_bytes=256)
            cs[m] = work.tile([P, P], U8, name="cs", tag="cs", bufs=4, align_bytes=256)
            nc.vector.quantize_mx(
                out=cq[m][:].bitcast(FP8X4), scales=cs[m][:], in_=cg[m][:].rearrange("p r j -> p (r j)")
            )

        bank, unit, pending = {}, {}, []
        outs = [o[0].rearrange("(m p) h d -> m p h d", p=P) for o in (out_0, out_1)]

        def new_bank(key):
            bank[key] = psum.tile([P, NB], F32, name="ob", tag="ob", bufs=BUFS["ob"])
            return bank[key]

        def rope_pass(key, g):
            kind, m, t, h0, nh = key
            cols = slice(h0 * DH, (h0 + nh) * DH)
            nc.tensor.matmul_mx(
                out=bank[key][:, 0 : nh * DH], lhsT=xq[m][:, g, :].bitcast(FP8X4), lhsT_scale=xs[m][:, g, :],
                rhs=wr[t][:, g, cols].bitcast(FP8X4), rhs_scale=wrs[t][4 * g : P, cols],
                start=(g == 0), stop=(g == G - 1),
            )

        def produce(key):
            kind, m, t, h0, nh = key
            new_bank(key)
            if kind == "r":
                for g in range(G):
                    rope_pass(key, g)
            else:
                cols = slice(h0 * DH, (h0 + nh) * DH)
                nc.tensor.matmul_mx(
                    out=bank[key][:], lhsT=cq[m][:].bitcast(FP8X4), lhsT_scale=cs[m][:],
                    rhs=wd[t][:, cols].bitcast(FP8X4), rhs_scale=wds[4 * t : P, cols],
                    start=True, stop=True,
                )

        def consume(key):
            kind, m, t, h0, nh = key
            if key[:3] not in unit:
                unit[key[:3]] = (
                    work.tile([P, 2, 2 * HB, R], F32, name="ab", tag="ab", bufs=4),
                    work.tile([P, 2 * HB, DH], F32, name="ot", tag="ot", bufs=6),
                )
            ab, ot = unit[key[:3]]
            heads = bank[key][:, 0 : nh * DH].rearrange("p (h d) -> p h d", h=nh)
            hs = slice(h0, h0 + nh)
            nc.vector.tensor_tensor(
                out=ab[:, :, hs, :],
                in0=heads[:, :, R:DH].unsqueeze(1).to_broadcast([P, 2, nh, R]),
                in1=tab[:, m].unsqueeze(2).to_broadcast([P, 2, nh, R]),
                op=ALU.mult,
            )
            nc.scalar.copy(out=ot[:, hs, 0:R], in_=heads[:, :, 0:R])
            while pending:
                finish(*pending.pop())
            if key[:3] == ("r", MT - 1, 1):
                part = hs
            elif h0 == HB:
                part = slice(0, 2 * HB)
            else:
                return
            if key[:3] in VADDS:
                pending.append((nc.vector, key, part))
            else:
                finish(nc.gpsimd, key, part)

        def finish(eng, key, part):
            kind, m, t = key[:3]
            ab, ot = unit[key[:3]]
            eng.tensor_tensor(out=ot[:, part, R : R + HALF], in0=ab[:, 0, part, 0:HALF], in1=ab[:, 1, part, HALF:R], op=ALU.add)
            eng.tensor_tensor(out=ot[:, part, R + HALF : DH], in0=ab[:, 0, part, HALF:R], in1=ab[:, 1, part, 0:HALF], op=ALU.add)
            f0 = 8 * (kind == "r") + part.start
            nc.sync.dma_start(out=outs[t][m, :, f0 : f0 + part.stop - part.start, :], in_=ot[:, part, :])

        def warm_up(n):
            wb = psum.tile([P, 512], F32, name="wb", tag="cc", bufs=BUFS["cc"])
            for w in range(n):
                nc.tensor.matmul(wb[:], lhsT=dummy[:, 0:P], rhs=dummy[:], start=True, stop=True)

        warm_up(WARM)
        table_part_1()
        table_part_2()
        table_part_3()
        table_part_4()
        cast(0, "v", 0, 512)
        cast(0, "s", 512, 1024)
        cast(0, "v", 1024, 1536)
        cast(0, "s", 1536, 2048)
        table_part_5()
        turn(0, 0)
        turn(0, 1)
        scale(0, 0)
        scale(0, 1)
        quant(0, 0, 1)
        scale(0, 2)
        quant(0, 1, 2)
        cast(1, "s", 0, 1024)
        cast(1, "s", 1024, 2048)
        cast(2, "s", 0, 1024)
        cast(2, "s", 1024, 2048)
        turn(1, 0)
        turn(1, 1, "ob")
        scale(0, 3)
        quant(0, 2, 3)
        scale(1, 0)
        quant(0, 3, 4)
        latent(0)
        latent_out(0)
        turn(2, 0)
        scale(1, 1)
        scale(1, 2)
        quant(1, 0, 2)
        scale(1, 3)
        b0, b1 = ("r", 0, 0, 0, HB), ("r", 0, 0, HB, HB)
        new_bank(b0)
        new_bank(b1)
        for g in (0, 1):
            rope_pass(b0, g)
            rope_pass(b1, g)
        latent_turn(0)
        turn(2, 1)
        scale(2, 0)
        quant(1, 2, 4)
        latent(1)
        latent_out(1)
        for g in (2, 3):
            rope_pass(b0, g)
            rope_pass(b1, g)
        scale(2, 1)
        latent_quant(0)
        scale(2, 2)
        scale(2, 3)
        cast(3, "s", 0, 1024)
        cast(3, "s", 1024, 2048)
        todo = [
            ("r10", [lambda: quant(2, 0, 4)]),
            ("r10", [lambda: latent_turn(1), lambda: turn(3, 0), lambda: turn(3, 1), lambda: latent_quant(1)]),
            ("d00", [lambda: scale(3, 0), lambda: latent(2), lambda: latent_out(2)]),
            ("r20", [lambda: scale(3, 1)]),
            ("d00", [lambda: latent_turn(2)]),
            ("r20", [lambda: scale(3, 2)]),
            ("d01", [lambda: latent_quant(2)]),
            ("d01", [lambda: scale(3, 3)]),
            ("r01", []),
            ("d10", [lambda: quant(3, 0, 4)]),
            ("r01", []),
            ("d10", [lambda: latent(3), lambda: latent_out(3)]),
            ("r11", []),
            ("d11", [lambda: latent_turn(3)]),
            ("r11", []),
            ("d11", [lambda: latent_quant(3)]),
            ("r21", []),
            ("d20", []),
            ("d20", []),
            ("r21", []),
            ("d21", []),
            ("d21", []),
            ("r30", []),
            ("d30", []),
            ("d30", []),
            ("r30", []),
            ("d31", []),
            ("d31", []),
            ("r31", []),
            ("r31a", []),
            ("r31b", []),
        ]
        seq = [b0, b1]
        seen = {}
        lag = 2
        for code, before in todo:
            for step in before:
                step()
            unit_key = (code[0], int(code[1]), int(code[2]))
            h0 = seen.setdefault(unit_key, 0)
            nh = 2 if len(code) > 3 else HB
            seen[unit_key] = h0 + nh
            key = unit_key + (h0, nh)
            produce(key)
            seq.append(key)
            consume(seq[len(seq) - 1 - lag])
        for i in range(lag):
            consume(seq[len(seq) - lag + i])
        while pending:
            finish(*pending.pop())
